import numpy as np
import ml_dtypes


def mxq(x, axis, fmt="e4m3"):
    dtype, down = {"e4m3": (ml_dtypes.float8_e4m3fn, 7), "e5m2": (ml_dtypes.float8_e5m2, 14)}[fmt]
    v = np.moveaxis(np.asarray(x, np.float32).astype(ml_dtypes.bfloat16).astype(np.float64), axis, -1)
    blocks = v.reshape(v.shape[:-1] + (-1, 32))
    amax = np.abs(blocks).max(-1, keepdims=True)
    byte = np.maximum(np.where(amax > 0, np.frexp(amax)[1] - 1 + 127, 0) - down, 1)
    scale = np.exp2(byte - 127.0)
    codes = (blocks / scale).astype(np.float32).astype(dtype).astype(np.float64)
    return np.moveaxis((codes * scale).reshape(v.shape), -1, axis)


WIDE = False


def mx_kscale(k):
    if not WIDE:
        return np.ones(k)
    levels = np.array([10, -10, 5, -5, 0])
    a = np.random.permutation(np.resize(levels, k // 512 * 4)).reshape(k // 512, 4)
    idx = np.arange(k)
    return np.exp2(a[idx // 512, idx % 128 // 32])


BF16 = ml_dtypes.bfloat16


def bf(x):
    return np.asarray(x, np.float32).astype(BF16)


def f64(x):
    return np.asarray(x).astype(np.float64)


B, S, D, QC, KVC, FF = 1, 512, 1024, 8, 2, 4096
EPS = 1e-5


def rmsnorm(u, w):
    return u / np.sqrt(np.square(u).mean(-1, keepdims=True) + EPS) * w


def setup_inputs():
    s = mx_kscale(D)
    t = np.exp2(np.round(np.log2(mx_kscale(FF)) / 2))
    return {"h_attn": bf(np.random.standard_normal((B, S, D)) * 1.3),
            "norm2_w": bf((1.0 + 0.1 * np.random.standard_normal(D)) * s),
            "ffn_wk": bf(np.random.standard_normal((D, FF)) / np.sqrt(D) / s[:, None] * t),
            "ffn_wv": bf(np.random.standard_normal((FF, D)) / np.sqrt(FF) / (t * t)[:, None])}


def reference(h_attn, norm2_w, ffn_wk, ffn_wv):
    h = f64(h_attn)
    hn = rmsnorm(h, f64(norm2_w))
    k = np.square(np.maximum(mxq(hn, 2, "e4m3") @ mxq(f64(ffn_wk), 0, "e4m3"), 0.0))
    return h + (mxq(k, 2, "e4m3") @ mxq(f64(ffn_wv), 0, "e4m3"))

@@ -1,0 +1,202 @@
+from contextlib import ExitStack
+
+import concourse.mybir as mybir
+from concourse.masks import make_identity
+
+F32 = mybir.dt.float32
+BF16 = mybir.dt.bfloat16
+U32 = mybir.dt.uint32
+U8 = mybir.dt.uint8
+FP8X4 = mybir.dt.float8_e4m3fn_x4
+ACT = mybir.ActivationFunctionType
+ALU = mybir.AluOpType
+
+P = 128
+PACK = 4
+K_PASS = P * PACK
+
+TOKENS = 512
+D_MODEL = 1024
+D_FF = 4096
+EPS = 1e-5
+
+TOK_TILES = TOKENS // P
+D_PASSES = D_MODEL // K_PASS
+FF_GROUPS = D_FF // K_PASS
+BANK = 512
+OUT_HALVES = D_MODEL // BANK
+WK_LOAD_COLS = 1024
+GROUPS_PER_LOAD = WK_LOAD_COLS // K_PASS
+RUN = 4
+WV_VECTOR_COLS = 256
+
+FLOPS = 2 * 2 * TOKENS * D_MODEL * D_FF
+
+
+def regroup(copy, grouped, rows):
+    copy(
+        out=grouped.rearrange("p (c i) t -> p c t i", i=RUN),
+        in_=rows.rearrange("p t (c i) -> p c t i", i=RUN),
+    )
+
+
+def tile_block_pc_kernel(tc, h_attn, norm2_w, ffn_wk, ffn_wv, out):
+    nc = tc.nc
+    h_rows = h_attn.flatten_outer_dims().rearrange("(n p) d -> n p d", p=P)
+    out_rows = out.flatten_outer_dims().rearrange("(n p) d -> n p d", p=P)
+    wk_rows = ffn_wk.rearrange("(c t p) f -> c p t f", t=PACK, p=P)
+    wv_rows = ffn_wv.rearrange("(g t p) d -> g p t d", t=PACK, p=P)
+
+    with ExitStack() as ctx:
+        keep = ctx.enter_context(tc.tile_pool(name="keep", bufs=1))
+        loads = ctx.enter_context(tc.tile_pool(name="loads", bufs=6))
+        work = ctx.enter_context(tc.tile_pool(name="work", bufs=2))
+        codes = ctx.enter_context(tc.tile_pool(name="codes", bufs=3))
+        results = ctx.enter_context(tc.tile_pool(name="results", bufs=4))
+        psum = ctx.enter_context(tc.psum_pool(name="psum", bufs=4))
+
+        gain_row = keep.tile([P, D_MODEL], BF16)
+        nc.vector.memset(gain_row[:], 0.0)
+        nc.sync.dma_start(out=gain_row[0:1, :], in_=norm2_w.rearrange("(o d) -> o d", o=1))
+        h_sb = keep.tile([P, TOK_TILES, D_MODEL], BF16)
+        for n in range(TOK_TILES):
+            nc.sync.dma_start(out=h_sb[:, n, :], in_=h_rows[n])
+
+        identity = keep.tile([P, P], BF16)
+        make_identity(nc, identity[:])
+        ones = keep.tile([P, P], BF16)
+        nc.vector.memset(ones[:], 1.0)
+        eps = keep.tile([P, 1], F32)
+        nc.vector.memset(eps[:], EPS)
+        table_warm = keep.tile([P, 1], F32)
+        nc.scalar.activation(out=table_warm[:], in_=eps[:], func=ACT.Sqrt)
+
+        gain = keep.tile([P, D_MODEL], F32)
+        for half in range(D_MODEL // BANK):
+            cols = slice(half * BANK, (half + 1) * BANK)
+            gain_ps = psum.tile([P, BANK], F32, tag="bank")
+            nc.tensor.matmul(out=gain_ps[:], lhsT=ones[:], rhs=gain_row[:, cols], start=True, stop=True)
+            nc.vector.tensor_copy(out=gain[:, cols], in_=gain_ps[:])
+
+        sum_sq = keep.tile([P, TOK_TILES], F32)
+        rms = keep.tile([P, TOK_TILES], F32)
+        inv_rms = keep.tile([P, TOK_TILES], F32)
+        hn_grouped = keep.tile([P, D_PASSES, TOKENS, PACK], BF16, align_bytes=64)
+        for n in range(TOK_TILES):
+            one = slice(n, n + 1)
+            squares = work.tile([P, D_MODEL], BF16)
+            nc.scalar.activation(out=squares[:], in_=h_sb[:, n, :], func=ACT.Square, accum_out=sum_sq[:, one])
+            nc.scalar.activation(
+                out=rms[:, one], in_=sum_sq[:, one], func=ACT.Sqrt, bias=eps[:], scale=1.0 / D_MODEL
+            )
+            nc.vector.reciprocal(out=inv_rms[:, one], in_=rms[:, one])
+            hn = work.tile([P, D_MODEL], BF16)
+            nc.vector.scalar_tensor_tensor(
+                out=hn[:], in0=h_sb[:, n, :], scalar=inv_rms[:, one], in1=gain[:], op0=ALU.mult, op1=ALU.mult
+            )
+            hn_t = psum.tile([P, D_PASSES, PACK, P], BF16, tag="bank")
+            for c in range(D_PASSES):
+                for t in range(PACK):
+                    first = c * K_PASS + t * P
+                    nc.tensor.transpose(hn_t[:, c, t, :], hn[:, first : first + P], identity[:])
+            nc.scalar.copy(
+                out=hn_grouped[:, :, n * P : (n + 1) * P, :], in_=hn_t[:].rearrange("p c t k -> p c k t")
+            )
+        hn_codes = keep.tile([P, D_PASSES, TOKENS], U32, align_bytes=64)
+        hn_scales = keep.tile([P, D_PASSES, TOKENS], U8, align_bytes=64)
+        nc.vector.quantize_mx(
+            out=hn_codes[:].rearrange("p c k -> p (c k)").bitcast(FP8X4),
+            scales=hn_scales[:].rearrange("p c k -> p (c k)"),
+            in_=hn_grouped[:].rearrange("p c k t -> p (c k t)"),
+        )
+
+        k_codes = keep.tile([P, FF_GROUPS, TOKENS], U32, align_bytes=64)
+        k_scales = keep.tile([P, FF_GROUPS, TOKENS], U8, align_bytes=64)
+
+        def hidden_group(g, wk_raw, cols):
+            wk_grouped = work.tile([P, D_PASSES, K_PASS, PACK], BF16, align_bytes=64)
+            for c in range(D_PASSES):
+                regroup(nc.vector.tensor_copy, wk_grouped[:, c], wk_raw[c][:, :, cols])
+            wk_codes = codes.tile([P, D_PASSES, K_PASS], U32, align_bytes=64)
+            wk_scales = codes.tile([P, D_PASSES, K_PASS], U8, align_bytes=64)
+            nc.vector.quantize_mx(
+                out=wk_codes[:].rearrange("p c f -> p (c f)").bitcast(FP8X4),
+                scales=wk_scales[:].rearrange("p c f -> p (c f)"),
+                in_=wk_grouped[:].rearrange("p c f t -> p (c f t)"),
+            )
+            relu = work.tile([P, TOKENS, PACK], F32)
+            for n in range(TOK_TILES):
+                toks = slice(n * P, (n + 1) * P)
+                pre = psum.tile([P, PACK, P], F32, tag="bank")
+                for t in range(PACK):
+                    units = slice(t * P, (t + 1) * P)
+                    for c in range(D_PASSES):
+                        nc.tensor.matmul_mx(
+                            out=pre[:, t, :],
+                            lhsT=wk_codes[:, c, units].bitcast(FP8X4),
+                            lhsT_scale=wk_scales[:, c, units],
+                            rhs=hn_codes[:, c, toks].bitcast(FP8X4),
+                            rhs_scale=hn_scales[:, c, toks],
+                            start=(c == 0),
+                            stop=(c == D_PASSES - 1),
+                        )
+                nc.scalar.activation(out=relu[:, toks, :], in_=pre[:].rearrange("p t k -> p k t"), func=ACT.Relu)
+            k_grouped = work.tile([P, TOKENS, PACK], BF16, align_bytes=64)
+            nc.scalar.activation(out=k_grouped[:], in_=relu[:], func=ACT.Square)
+            nc.vector.quantize_mx(
+                out=k_codes[:, g, :].bitcast(FP8X4),
+                scales=k_scales[:, g, :],
+                in_=k_grouped[:].rearrange("p k t -> p (k t)"),
+            )
+
+        def add_group_to_sums(g, half, sums):
+            wv_raw = loads.tile([P, PACK, BANK], BF16)
+            nc.sync.dma_start(out=wv_raw[:], in_=wv_rows[g, :, :, half * BANK : (half + 1) * BANK])
+            wv_grouped = work.tile([P, BANK, PACK], BF16, align_bytes=64)
+            regroup(nc.vector.tensor_copy, wv_grouped[:, :WV_VECTOR_COLS, :], wv_raw[:, :, :WV_VECTOR_COLS])
+            regroup(nc.scalar.copy, wv_grouped[:, WV_VECTOR_COLS:, :], wv_raw[:, :, WV_VECTOR_COLS:])
+            wv_codes = codes.tile([P, BANK], U32, align_bytes=64)
+            wv_scales = codes.tile([P, BANK], U8, align_bytes=64)
+            nc.vector.quantize_mx(
+                out=wv_codes[:].bitcast(FP8X4),
+                scales=wv_scales[:],
+                in_=wv_grouped[:].rearrange("p d t -> p (d t)"),
+            )
+            for n in range(TOK_TILES):
+                toks = slice(n * P, (n + 1) * P)
+                nc.tensor.matmul_mx(
+                    out=sums[n][:],
+                    lhsT=k_codes[:, g, toks].bitcast(FP8X4),
+                    lhsT_scale=k_scales[:, g, toks],
+                    rhs=wv_codes[:].bitcast(FP8X4),
+                    rhs_scale=wv_scales[:],
+                    start=(g == 0),
+                    stop=(g == FF_GROUPS - 1),
+                )
+
+        def add_residual_and_store(half, sums):
+            cols = slice(half * BANK, (half + 1) * BANK)
+            for n in range(TOK_TILES):
+                result = results.tile([P, BANK], F32)
+                nc.vector.tensor_tensor(out=result[:], in0=sums[n][:], in1=h_sb[:, n, cols], op=ALU.add)
+                nc.sync.dma_start(out=out_rows[n][:, cols], in_=result[:])
+
+        sums = [psum.tile([P, BANK], F32, tag="sums", name="sums%d" % n) for n in range(TOK_TILES)]
+        for load in range(D_FF // WK_LOAD_COLS):
+            wk_raw = []
+            for c in range(D_PASSES):
+                wk_part = loads.tile([P, PACK, WK_LOAD_COLS], BF16)
+                nc.sync.dma_start(
+                    out=wk_part[:], in_=wk_rows[c, :, :, load * WK_LOAD_COLS : (load + 1) * WK_LOAD_COLS]
+                )
+                wk_raw.append(wk_part)
+            for s in range(GROUPS_PER_LOAD):
+                g = load * GROUPS_PER_LOAD + s
+                hidden_group(g, wk_raw, slice(s * K_PASS, (s + 1) * K_PASS))
+                add_group_to_sums(g, 0, sums)
+        add_residual_and_store(0, sums)
+
+        sums = [psum.tile([P, BANK], F32, tag="bank", name="sums%d" % n) for n in range(TOK_TILES)]
+        for g in range(FF_GROUPS):
+            add_group_to_sums(g, 1, sums)
+        add_residual_and_store(1, sums)

@@ -25,8 +25,6 @@ D_PASSES = D_MODEL // K_PASS
 FF_GROUPS = D_FF // K_PASS
 BANK = 512
 OUT_HALVES = D_MODEL // BANK
-WK_LOAD_COLS = 1024
-GROUPS_PER_LOAD = WK_LOAD_COLS // K_PASS
 RUN = 4
 WV_VECTOR_COLS = 256
 
@@ -44,14 +42,17 @@ def tile_block_pc_kernel(tc, h_attn, norm2_w, ffn_wk, ffn_wv, out):
     nc = tc.nc
     h_rows = h_attn.flatten_outer_dims().rearrange("(n p) d -> n p d", p=P)
     out_rows = out.flatten_outer_dims().rearrange("(n p) d -> n p d", p=P)
-    wk_rows = ffn_wk.rearrange("(c t p) f -> c p t f", t=PACK, p=P)
+    wk_rows = ffn_wk.rearrange("(ct p) f -> p ct f", p=P)
     wv_rows = ffn_wv.rearrange("(g t p) d -> g p t d", t=PACK, p=P)
 
     with ExitStack() as ctx:
         keep = ctx.enter_context(tc.tile_pool(name="keep", bufs=1))
-        loads = ctx.enter_context(tc.tile_pool(name="loads", bufs=6))
+        wk_loads = ctx.enter_context(tc.tile_pool(name="wk_loads", bufs=4))
+        wv_loads = ctx.enter_context(tc.tile_pool(name="wv_loads", bufs=FF_GROUPS))
+        grouped = ctx.enter_context(tc.tile_pool(name="grouped", bufs=3))
+        wk_quantised = ctx.enter_context(tc.tile_pool(name="wk_quantised", bufs=3))
+        wv_quantised = ctx.enter_context(tc.tile_pool(name="wv_quantised", bufs=FF_GROUPS))
         work = ctx.enter_context(tc.tile_pool(name="work", bufs=2))
-        codes = ctx.enter_context(tc.tile_pool(name="codes", bufs=3))
         results = ctx.enter_context(tc.tile_pool(name="results", bufs=4))
         psum = ctx.enter_context(tc.psum_pool(name="psum", bufs=4))
 
@@ -81,7 +82,9 @@ def tile_block_pc_kernel(tc, h_attn, norm2_w, ffn_wk, ffn_wv, out):
         sum_sq = keep.tile([P, TOK_TILES], F32)
         rms = keep.tile([P, TOK_TILES], F32)
         inv_rms = keep.tile([P, TOK_TILES], F32)
-        hn_grouped = keep.tile([P, D_PASSES, TOKENS, PACK], BF16, align_bytes=64)
+        hn_grouped = keep.tile([P, TOK_TILES, D_PASSES, P, PACK], BF16, align_bytes=64)
+        hn_codes = keep.tile([P, TOK_TILES, D_PASSES, P], U32, align_bytes=64)
+        hn_scales = keep.tile([P, TOK_TILES, D_PASSES, P], U8, align_bytes=64)
         for n in range(TOK_TILES):
             one = slice(n, n + 1)
             squares = work.tile([P, D_MODEL], BF16)
@@ -99,26 +102,24 @@ def tile_block_pc_kernel(tc, h_attn, norm2_w, ffn_wk, ffn_wv, out):
                 for t in range(PACK):
                     first = c * K_PASS + t * P
                     nc.tensor.transpose(hn_t[:, c, t, :], hn[:, first : first + P], identity[:])
-            nc.scalar.copy(
-                out=hn_grouped[:, :, n * P : (n + 1) * P, :], in_=hn_t[:].rearrange("p c t k -> p c k t")
+            nc.scalar.copy(out=hn_grouped[:, n], in_=hn_t[:].rearrange("p c t k -> p c k t"))
+            nc.vector.quantize_mx(
+                out=hn_codes[:, n].rearrange("p c k -> p (c k)").bitcast(FP8X4),
+                scales=hn_scales[:, n].rearrange("p c k -> p (c k)"),
+                in_=hn_grouped[:, n].rearrange("p c k t -> p (c k t)"),
             )
-        hn_codes = keep.tile([P, D_PASSES, TOKENS], U32, align_bytes=64)
-        hn_scales = keep.tile([P, D_PASSES, TOKENS], U8, align_bytes=64)
-        nc.vector.quantize_mx(
-            out=hn_codes[:].rearrange("p c k -> p (c k)").bitcast(FP8X4),
-            scales=hn_scales[:].rearrange("p c k -> p (c k)"),
-            in_=hn_grouped[:].rearrange("p c k t -> p (c k t)"),
-        )
 
         k_codes = keep.tile([P, FF_GROUPS, TOKENS], U32, align_bytes=64)
         k_scales = keep.tile([P, FF_GROUPS, TOKENS], U8, align_bytes=64)
 
-        def hidden_group(g, wk_raw, cols):
-            wk_grouped = work.tile([P, D_PASSES, K_PASS, PACK], BF16, align_bytes=64)
+        def hidden_group(g):
+            wk_raw = wk_loads.tile([P, D_PASSES * PACK, K_PASS], BF16)
+            nc.sync.dma_start(out=wk_raw[:], in_=wk_rows[:, :, g * K_PASS : (g + 1) * K_PASS])
+            wk_grouped = grouped.tile([P, D_PASSES, K_PASS, PACK], BF16, align_bytes=64)
             for c in range(D_PASSES):
-                regroup(nc.vector.tensor_copy, wk_grouped[:, c], wk_raw[c][:, :, cols])
-            wk_codes = codes.tile([P, D_PASSES, K_PASS], U32, align_bytes=64)
-            wk_scales = codes.tile([P, D_PASSES, K_PASS], U8, align_bytes=64)
+                regroup(nc.vector.tensor_copy, wk_grouped[:, c], wk_raw[:, c * PACK : (c + 1) * PACK, :])
+            wk_codes = wk_quantised.tile([P, D_PASSES, K_PASS], U32, align_bytes=64)
+            wk_scales = wk_quantised.tile([P, D_PASSES, K_PASS], U8, align_bytes=64)
             nc.vector.quantize_mx(
                 out=wk_codes[:].rearrange("p c f -> p (c f)").bitcast(FP8X4),
                 scales=wk_scales[:].rearrange("p c f -> p (c f)"),
@@ -135,13 +136,13 @@ def tile_block_pc_kernel(tc, h_attn, norm2_w, ffn_wk, ffn_wv, out):
                             out=pre[:, t, :],
                             lhsT=wk_codes[:, c, units].bitcast(FP8X4),
                             lhsT_scale=wk_scales[:, c, units],
-                            rhs=hn_codes[:, c, toks].bitcast(FP8X4),
-                            rhs_scale=hn_scales[:, c, toks],
+                            rhs=hn_codes[:, n, c, :].bitcast(FP8X4),
+                            rhs_scale=hn_scales[:, n, c, :],
                             start=(c == 0),
                             stop=(c == D_PASSES - 1),
                         )
                 nc.scalar.activation(out=relu[:, toks, :], in_=pre[:].rearrange("p t k -> p k t"), func=ACT.Relu)
-            k_grouped = work.tile([P, TOKENS, PACK], BF16, align_bytes=64)
+            k_grouped = grouped.tile([P, TOKENS, PACK], BF16, align_bytes=64)
             nc.scalar.activation(out=k_grouped[:], in_=relu[:], func=ACT.Square)
             nc.vector.quantize_mx(
                 out=k_codes[:, g, :].bitcast(FP8X4),
@@ -150,13 +151,13 @@ def tile_block_pc_kernel(tc, h_attn, norm2_w, ffn_wk, ffn_wv, out):
             )
 
         def add_group_to_sums(g, half, sums):
-            wv_raw = loads.tile([P, PACK, BANK], BF16)
+            wv_raw = wv_loads.tile([P, PACK, BANK], BF16)
             nc.sync.dma_start(out=wv_raw[:], in_=wv_rows[g, :, :, half * BANK : (half + 1) * BANK])
-            wv_grouped = work.tile([P, BANK, PACK], BF16, align_bytes=64)
+            wv_grouped = grouped.tile([P, BANK, PACK], BF16, align_bytes=64)
             regroup(nc.vector.tensor_copy, wv_grouped[:, :WV_VECTOR_COLS, :], wv_raw[:, :, :WV_VECTOR_COLS])
             regroup(nc.scalar.copy, wv_grouped[:, WV_VECTOR_COLS:, :], wv_raw[:, :, WV_VECTOR_COLS:])
-            wv_codes = codes.tile([P, BANK], U32, align_bytes=64)
-            wv_scales = codes.tile([P, BANK], U8, align_bytes=64)
+            wv_codes = wv_quantised.tile([P, BANK], U32, align_bytes=64)
+            wv_scales = wv_quantised.tile([P, BANK], U8, align_bytes=64)
             nc.vector.quantize_mx(
                 out=wv_codes[:].bitcast(FP8X4),
                 scales=wv_scales[:],
@@ -182,18 +183,9 @@ def tile_block_pc_kernel(tc, h_attn, norm2_w, ffn_wk, ffn_wv, out):
                 nc.sync.dma_start(out=out_rows[n][:, cols], in_=result[:])
 
         sums = [psum.tile([P, BANK], F32, tag="sums", name="sums%d" % n) for n in range(TOK_TILES)]
-        for load in range(D_FF // WK_LOAD_COLS):
-            wk_raw = []
-            for c in range(D_PASSES):
-                wk_part = loads.tile([P, PACK, WK_LOAD_COLS], BF16)
-                nc.sync.dma_start(
-                    out=wk_part[:], in_=wk_rows[c, :, :, load * WK_LOAD_COLS : (load + 1) * WK_LOAD_COLS]
-                )
-                wk_raw.append(wk_part)
-            for s in range(GROUPS_PER_LOAD):
-                g = load * GROUPS_PER_LOAD + s
-                hidden_group(g, wk_raw, slice(s * K_PASS, (s + 1) * K_PASS))
-                add_group_to_sums(g, 0, sums)
+        for g in range(FF_GROUPS):
+            hidden_group(g)
+            add_group_to_sums(g, 0, sums)
         add_residual_and_store(0, sums)
 
         sums = [psum.tile([P, BANK], F32, tag="bank", name="sums%d" % n) for n in range(TOK_TILES)]

@@ -26,7 +26,7 @@ FF_GROUPS = D_FF // K_PASS
 BANK = 512
 OUT_HALVES = D_MODEL // BANK
 RUN = 4
-WV_VECTOR_COLS = 256
+PIECE = 256
 
 FLOPS = 2 * 2 * TOKENS * D_MODEL * D_FF
 
@@ -117,7 +117,9 @@ def tile_block_pc_kernel(tc, h_attn, norm2_w, ffn_wk, ffn_wv, out):
             nc.sync.dma_start(out=wk_raw[:], in_=wk_rows[:, :, g * K_PASS : (g + 1) * K_PASS])
             wk_grouped = grouped.tile([P, D_PASSES, K_PASS, PACK], BF16, align_bytes=64)
             for c in range(D_PASSES):
-                regroup(nc.vector.tensor_copy, wk_grouped[:, c], wk_raw[:, c * PACK : (c + 1) * PACK, :])
+                for first in range(0, K_PASS, PIECE):
+                    cols = slice(first, first + PIECE)
+                    regroup(nc.any.tensor_copy, wk_grouped[:, c, cols, :], wk_raw[:, c * PACK : (c + 1) * PACK, cols])
             wk_codes = wk_quantised.tile([P, D_PASSES, K_PASS], U32, align_bytes=64)
             wk_scales = wk_quantised.tile([P, D_PASSES, K_PASS], U8, align_bytes=64)
             nc.vector.quantize_mx(
@@ -154,8 +156,9 @@ def tile_block_pc_kernel(tc, h_attn, norm2_w, ffn_wk, ffn_wv, out):
             wv_raw = wv_loads.tile([P, PACK, BANK], BF16)
             nc.sync.dma_start(out=wv_raw[:], in_=wv_rows[g, :, :, half * BANK : (half + 1) * BANK])
             wv_grouped = grouped.tile([P, BANK, PACK], BF16, align_bytes=64)
-            regroup(nc.vector.tensor_copy, wv_grouped[:, :WV_VECTOR_COLS, :], wv_raw[:, :, :WV_VECTOR_COLS])
-            regroup(nc.scalar.copy, wv_grouped[:, WV_VECTOR_COLS:, :], wv_raw[:, :, WV_VECTOR_COLS:])
+            for first in range(0, BANK, PIECE):
+                cols = slice(first, first + PIECE)
+                regroup(nc.any.tensor_copy, wv_grouped[:, cols, :], wv_raw[:, :, cols])
             wv_codes = wv_quantised.tile([P, BANK], U32, align_bytes=64)
             wv_scales = wv_quantised.tile([P, BANK], U8, align_bytes=64)
             nc.vector.quantize_mx(

@@ -26,7 +26,7 @@ FF_GROUPS = D_FF // K_PASS
 BANK = 512
 OUT_HALVES = D_MODEL // BANK
 RUN = 4
-PIECE = 256
+PIECE = 512
 
 FLOPS = 2 * 2 * TOKENS * D_MODEL * D_FF
 

@@ -26,7 +26,7 @@ FF_GROUPS = D_FF // K_PASS
 BANK = 512
 OUT_HALVES = D_MODEL // BANK
 RUN = 4
-PIECE = 512
+PIECE = 256
 
 FLOPS = 2 * 2 * TOKENS * D_MODEL * D_FF
 
@@ -112,7 +112,7 @@ def tile_block_pc_kernel(tc, h_attn, norm2_w, ffn_wk, ffn_wv, out):
         k_codes = keep.tile([P, FF_GROUPS, TOKENS], U32, align_bytes=64)
         k_scales = keep.tile([P, FF_GROUPS, TOKENS], U8, align_bytes=64)
 
-        def hidden_group(g):
+        def regroup_wk(g):
             wk_raw = wk_loads.tile([P, D_PASSES * PACK, K_PASS], BF16)
             nc.sync.dma_start(out=wk_raw[:], in_=wk_rows[:, :, g * K_PASS : (g + 1) * K_PASS])
             wk_grouped = grouped.tile([P, D_PASSES, K_PASS, PACK], BF16, align_bytes=64)
@@ -120,6 +120,9 @@ def tile_block_pc_kernel(tc, h_attn, norm2_w, ffn_wk, ffn_wv, out):
                 for first in range(0, K_PASS, PIECE):
                     cols = slice(first, first + PIECE)
                     regroup(nc.any.tensor_copy, wk_grouped[:, c, cols, :], wk_raw[:, c * PACK : (c + 1) * PACK, cols])
+            return wk_grouped
+
+        def hidden_group(g, wk_grouped):
             wk_codes = wk_quantised.tile([P, D_PASSES, K_PASS], U32, align_bytes=64)
             wk_scales = wk_quantised.tile([P, D_PASSES, K_PASS], U8, align_bytes=64)
             nc.vector.quantize_mx(
@@ -152,13 +155,16 @@ def tile_block_pc_kernel(tc, h_attn, norm2_w, ffn_wk, ffn_wv, out):
                 in_=k_grouped[:].rearrange("p k t -> p (k t)"),
             )
 
-        def add_group_to_sums(g, half, sums):
+        def regroup_wv(g, half):
             wv_raw = wv_loads.tile([P, PACK, BANK], BF16)
             nc.sync.dma_start(out=wv_raw[:], in_=wv_rows[g, :, :, half * BANK : (half + 1) * BANK])
             wv_grouped = grouped.tile([P, BANK, PACK], BF16, align_bytes=64)
             for first in range(0, BANK, PIECE):
                 cols = slice(first, first + PIECE)
                 regroup(nc.any.tensor_copy, wv_grouped[:, cols, :], wv_raw[:, :, cols])
+            return wv_grouped
+
+        def add_group_to_sums(g, wv_grouped, sums):
             wv_codes = wv_quantised.tile([P, BANK], U32, align_bytes=64)
             wv_scales = wv_quantised.tile([P, BANK], U8, align_bytes=64)
             nc.vector.quantize_mx(
@@ -185,13 +191,22 @@ def tile_block_pc_kernel(tc, h_attn, norm2_w, ffn_wk, ffn_wv, out):
                 nc.vector.tensor_tensor(out=result[:], in0=sums[n][:], in1=h_sb[:, n, cols], op=ALU.add)
                 nc.sync.dma_start(out=out_rows[n][:, cols], in_=result[:])
 
+        wk_grouped = regroup_wk(0)
+        wv_grouped = regroup_wv(0, 0)
         sums = [psum.tile([P, BANK], F32, tag="sums", name="sums%d" % n) for n in range(TOK_TILES)]
         for g in range(FF_GROUPS):
-            hidden_group(g)
-            add_group_to_sums(g, 0, sums)
+            wk_ready, wv_ready = wk_grouped, wv_grouped
+            if g + 1 < FF_GROUPS:
+                wk_grouped = regroup_wk(g + 1)
+            hidden_group(g, wk_ready)
+            wv_grouped = regroup_wv((g + 1) % FF_GROUPS, (g + 1) // FF_GROUPS)
+            add_group_to_sums(g, wv_ready, sums)
         add_residual_and_store(0, sums)
 
         sums = [psum.tile([P, BANK], F32, tag="bank", name="sums%d" % n) for n in range(TOK_TILES)]
         for g in range(FF_GROUPS):
-            add_group_to_sums(g, 1, sums)
+            wv_ready = wv_grouped
+            if g + 1 < FF_GROUPS:
+                wv_grouped = regroup_wv(g + 1, 1)
+            add_group_to_sums(g, wv_ready, sums)
         add_residual_and_store(1, sums)

from contextlib import ExitStack

import concourse.mybir as mybir
from concourse.masks import make_identity

F32 = mybir.dt.float32
BF16 = mybir.dt.bfloat16
U32 = mybir.dt.uint32
U8 = mybir.dt.uint8
FP8X4 = mybir.dt.float8_e4m3fn_x4
ACT = mybir.ActivationFunctionType
ALU = mybir.AluOpType

P = 128
PACK = 4
K_PASS = P * PACK

TOKENS = 512
D_MODEL = 1024
D_FF = 4096
EPS = 1e-5

TOK_TILES = TOKENS // P
D_PASSES = D_MODEL // K_PASS
FF_GROUPS = D_FF // K_PASS
BANK = 512
OUT_HALVES = D_MODEL // BANK
RUN = 4
PIECE = 256

FLOPS = 2 * 2 * TOKENS * D_MODEL * D_FF


def regroup(copy, grouped, rows):
    copy(
        out=grouped.rearrange("p (c i) t -> p c t i", i=RUN),
        in_=rows.rearrange("p t (c i) -> p c t i", i=RUN),
    )


def tile_block_pc_kernel(tc, h_attn, norm2_w, ffn_wk, ffn_wv, out):
    nc = tc.nc
    h_rows = h_attn.flatten_outer_dims().rearrange("(n p) d -> n p d", p=P)
    out_rows = out.flatten_outer_dims().rearrange("(n p) d -> n p d", p=P)
    wk_rows = ffn_wk.rearrange("(ct p) f -> p ct f", p=P)
    wv_rows = ffn_wv.rearrange("(g t p) d -> g p t d", t=PACK, p=P)

    with ExitStack() as ctx:
        keep = ctx.enter_context(tc.tile_pool(name="keep", bufs=1))
        wk_loads = ctx.enter_context(tc.tile_pool(name="wk_loads", bufs=4))
        wv_loads = ctx.enter_context(tc.tile_pool(name="wv_loads", bufs=FF_GROUPS))
        grouped = ctx.enter_context(tc.tile_pool(name="grouped", bufs=3))
        wk_quantised = ctx.enter_context(tc.tile_pool(name="wk_quantised", bufs=3))
        wv_quantised = ctx.enter_context(tc.tile_pool(name="wv_quantised", bufs=FF_GROUPS))
        work = ctx.enter_context(tc.tile_pool(name="work", bufs=2))
        results = ctx.enter_context(tc.tile_pool(name="results", bufs=4))
        psum = ctx.enter_context(tc.psum_pool(name="psum", bufs=4))

        gain_row = keep.tile([P, D_MODEL], BF16)
        nc.vector.memset(gain_row[:], 0.0)
        nc.sync.dma_start(out=gain_row[0:1, :], in_=norm2_w.rearrange("(o d) -> o d", o=1))
        h_sb = keep.tile([P, TOK_TILES, D_MODEL], BF16)
        for n in range(TOK_TILES):
            nc.sync.dma_start(out=h_sb[:, n, :], in_=h_rows[n])

        identity = keep.tile([P, P], BF16)
        make_identity(nc, identity[:])
        ones = keep.tile([P, P], BF16)
        nc.vector.memset(ones[:], 1.0)
        eps = keep.tile([P, 1], F32)
        nc.vector.memset(eps[:], EPS)
        table_warm = keep.tile([P, 1], F32)
        nc.scalar.activation(out=table_warm[:], in_=eps[:], func=ACT.Sqrt)

        gain = keep.tile([P, D_MODEL], F32)
        for half in range(D_MODEL // BANK):
            cols = slice(half * BANK, (half + 1) * BANK)
            gain_ps = psum.tile([P, BANK], F32, tag="bank")
            nc.tensor.matmul(out=gain_ps[:], lhsT=ones[:], rhs=gain_row[:, cols], start=True, stop=True)
            nc.vector.tensor_copy(out=gain[:, cols], in_=gain_ps[:])

        sum_sq = keep.tile([P, TOK_TILES], F32)
        rms = keep.tile([P, TOK_TILES], F32)
        inv_rms = keep.tile([P, TOK_TILES], F32)
        hn_grouped = keep.tile([P, TOK_TILES, D_PASSES, P, PACK], BF16, align_bytes=64)
        hn_codes = keep.tile([P, TOK_TILES, D_PASSES, P], U32, align_bytes=64)
        hn_scales = keep.tile([P, TOK_TILES, D_PASSES, P], U8, align_bytes=64)
        for n in range(TOK_TILES):
            one = slice(n, n + 1)
            squares = work.tile([P, D_MODEL], BF16)
            nc.scalar.activation(out=squares[:], in_=h_sb[:, n, :], func=ACT.Square, accum_out=sum_sq[:, one])
            nc.scalar.activation(
                out=rms[:, one], in_=sum_sq[:, one], func=ACT.Sqrt, bias=eps[:], scale=1.0 / D_MODEL
            )
            nc.vector.reciprocal(out=inv_rms[:, one], in_=rms[:, one])
            hn = work.tile([P, D_MODEL], BF16)
            nc.vector.scalar_tensor_tensor(
                out=hn[:], in0=h_sb[:, n, :], scalar=inv_rms[:, one], in1=gain[:], op0=ALU.mult, op1=ALU.mult
            )
            hn_t = psum.tile([P, D_PASSES, PACK, P], BF16, tag="bank")
            for c in range(D_PASSES):
                for t in range(PACK):
                    first = c * K_PASS + t * P
                    nc.tensor.transpose(hn_t[:, c, t, :], hn[:, first : first + P], identity[:])
            nc.scalar.copy(out=hn_grouped[:, n], in_=hn_t[:].rearrange("p c t k -> p c k t"))
            nc.vector.quantize_mx(
                out=hn_codes[:, n].rearrange("p c k -> p (c k)").bitcast(FP8X4),
                scales=hn_scales[:, n].rearrange("p c k -> p (c k)"),
                in_=hn_grouped[:, n].rearrange("p c k t -> p (c k t)"),
            )

        k_codes = keep.tile([P, FF_GROUPS, TOKENS], U32, align_bytes=64)
        k_scales = keep.tile([P, FF_GROUPS, TOKENS], U8, align_bytes=64)

        def regroup_wk(g):
            wk_raw = wk_loads.tile([P, D_PASSES * PACK, K_PASS], BF16)
            nc.sync.dma_start(out=wk_raw[:], in_=wk_rows[:, :, g * K_PASS : (g + 1) * K_PASS])
            wk_grouped = grouped.tile([P, D_PASSES, K_PASS, PACK], BF16, align_bytes=64)
            for c in range(D_PASSES):
                for first in range(0, K_PASS, PIECE):
                    cols = slice(first, first + PIECE)
                    regroup(nc.any.tensor_copy, wk_grouped[:, c, cols, :], wk_raw[:, c * PACK : (c + 1) * PACK, cols])
            return wk_grouped

        def hidden_group(g, wk_grouped):
            wk_codes = wk_quantised.tile([P, D_PASSES, K_PASS], U32, align_bytes=64)
            wk_scales = wk_quantised.tile([P, D_PASSES, K_PASS], U8, align_bytes=64)
            nc.vector.quantize_mx(
                out=wk_codes[:].rearrange("p c f -> p (c f)").bitcast(FP8X4),
                scales=wk_scales[:].rearrange("p c f -> p (c f)"),
                in_=wk_grouped[:].rearrange("p c f t -> p (c f t)"),
            )
            relu = work.tile([P, TOKENS, PACK], F32)
            for n in range(TOK_TILES):
                toks = slice(n * P, (n + 1) * P)
                pre = psum.tile([P, PACK, P], F32, tag="bank")
                for t in range(PACK):
                    units = slice(t * P, (t + 1) * P)
                    for c in range(D_PASSES):
                        nc.tensor.matmul_mx(
                            out=pre[:, t, :],
                            lhsT=wk_codes[:, c, units].bitcast(FP8X4),
                            lhsT_scale=wk_scales[:, c, units],
                            rhs=hn_codes[:, n, c, :].bitcast(FP8X4),
                            rhs_scale=hn_scales[:, n, c, :],
                            start=(c == 0),
                            stop=(c == D_PASSES - 1),
                        )
                nc.scalar.activation(out=relu[:, toks, :], in_=pre[:].rearrange("p t k -> p k t"), func=ACT.Relu)
            k_grouped = grouped.tile([P, TOKENS, PACK], BF16, align_bytes=64)
            nc.scalar.activation(out=k_grouped[:], in_=relu[:], func=ACT.Square)
            nc.vector.quantize_mx(
                out=k_codes[:, g, :].bitcast(FP8X4),
                scales=k_scales[:, g, :],
                in_=k_grouped[:].rearrange("p k t -> p (k t)"),
            )

        def regroup_wv(g, half):
            wv_raw = wv_loads.tile([P, PACK, BANK], BF16)
            nc.sync.dma_start(out=wv_raw[:], in_=wv_rows[g, :, :, half * BANK : (half + 1) * BANK])
            wv_grouped = grouped.tile([P, BANK, PACK], BF16, align_bytes=64)
            for first in range(0, BANK, PIECE):
                cols = slice(first, first + PIECE)
                regroup(nc.any.tensor_copy, wv_grouped[:, cols, :], wv_raw[:, :, cols])
            return wv_grouped

        def add_group_to_sums(g, wv_grouped, sums):
            wv_codes = wv_quantised.tile([P, BANK], U32, align_bytes=64)
            wv_scales = wv_quantised.tile([P, BANK], U8, align_bytes=64)
            nc.vector.quantize_mx(
                out=wv_codes[:].bitcast(FP8X4),
                scales=wv_scales[:],
                in_=wv_grouped[:].rearrange("p d t -> p (d t)"),
            )
            for n in range(TOK_TILES):
                toks = slice(n * P, (n + 1) * P)
                nc.tensor.matmul_mx(
                    out=sums[n][:],
                    lhsT=k_codes[:, g, toks].bitcast(FP8X4),
                    lhsT_scale=k_scales[:, g, toks],
                    rhs=wv_codes[:].bitcast(FP8X4),
                    rhs_scale=wv_scales[:],
                    start=(g == 0),
                    stop=(g == FF_GROUPS - 1),
                )

        def add_residual_and_store(half, sums):
            cols = slice(half * BANK, (half + 1) * BANK)
            for n in range(TOK_TILES):
                result = results.tile([P, BANK], F32)
                nc.vector.tensor_tensor(out=result[:], in0=sums[n][:], in1=h_sb[:, n, cols], op=ALU.add)
                nc.sync.dma_start(out=out_rows[n][:, cols], in_=result[:])

        wk_grouped = regroup_wk(0)
        wv_grouped = regroup_wv(0, 0)
        sums = [psum.tile([P, BANK], F32, tag="sums", name="sums%d" % n) for n in range(TOK_TILES)]
        for g in range(FF_GROUPS):
            wk_ready, wv_ready = wk_grouped, wv_grouped
            if g + 1 < FF_GROUPS:
                wk_grouped = regroup_wk(g + 1)
            hidden_group(g, wk_ready)
            wv_grouped = regroup_wv((g + 1) % FF_GROUPS, (g + 1) // FF_GROUPS)
            add_group_to_sums(g, wv_ready, sums)
        add_residual_and_store(0, sums)

        sums = [psum.tile([P, BANK], F32, tag="bank", name="sums%d" % n) for n in range(TOK_TILES)]
        for g in range(FF_GROUPS):
            wv_ready = wv_grouped
            if g + 1 < FF_GROUPS:
                wv_grouped = regroup_wv(g + 1, 1)
            add_group_to_sums(g, wv_ready, sums)
        add_residual_and_store(1, sums)
